import numpy as np
import ml_dtypes


def mxq(x, axis, fmt="e4m3"):
    dtype, down = {"e4m3": (ml_dtypes.float8_e4m3fn, 7), "e5m2": (ml_dtypes.float8_e5m2, 14)}[fmt]
    v = np.moveaxis(np.asarray(x, np.float32).astype(ml_dtypes.bfloat16).astype(np.float64), axis, -1)
    blocks = v.reshape(v.shape[:-1] + (-1, 32))
    amax = np.abs(blocks).max(-1, keepdims=True)
    byte = np.maximum(np.where(amax > 0, np.frexp(amax)[1] - 1 + 127, 0) - down, 1)
    scale = np.exp2(byte - 127.0)
    codes = (blocks / scale).astype(np.float32).astype(dtype).astype(np.float64)
    return np.moveaxis((codes * scale).reshape(v.shape), -1, axis)


WIDE = False


def mx_kscale(k):
    if not WIDE:
        return np.ones(k)
    levels = np.array([10, -10, 5, -5, 0])
    a = np.random.permutation(np.resize(levels, k // 512 * 4)).reshape(k // 512, 4)
    idx = np.arange(k)
    return np.exp2(a[idx // 512, idx % 128 // 32])


BF16 = ml_dtypes.bfloat16


def bf(x):
    return np.asarray(x, np.float32).astype(BF16)


def f64(x):
    return np.asarray(x).astype(np.float64)


B, C, H, W = 2, 1024, 16, 32
C2 = 2 * C
N = H * W


def sigmoid(v):
    return 1.0 / (1.0 + np.exp(-v))


def setup_inputs():
    s = mx_kscale(C2)
    t = mx_kscale(C)
    return {"hsi": bf(np.random.standard_normal((B, C, H, W)) * s[:C][None, :, None, None]),
            "msi": bf(np.random.standard_normal((B, C, H, W)) * s[C:][None, :, None, None]),
            "att1": bf(np.random.standard_normal((B, C, H, W)) * 0.5 * t[None, :, None, None]),
            "att2": bf(np.random.standard_normal((B, C, H, W)) * 0.5 * t[None, :, None, None]),
            "wg": bf(np.random.standard_normal((C, C2)) / np.sqrt(C2) / s[None, :]),
            "bg": bf(np.random.standard_normal(C) * 0.2),
            "wp": bf(np.random.standard_normal((C, C)) * 2.0 / np.sqrt(C) / t[None, :]),
            "bp": bf(np.random.standard_normal(C) * 0.1)}


def reference(hsi, msi, att1, att2, wg, bg, wp, bp):
    x = np.concatenate([f64(hsi), f64(msi)], axis=1).reshape(B, C2, N)
    g = sigmoid((mxq(f64(wg), 1, "e4m3") @ mxq(x, 1, "e4m3")) + f64(bg)[None, :, None])
    fused = g * f64(att1).reshape(B, C, N) + (1.0 - g) * f64(att2).reshape(B, C, N)
    y = (mxq(f64(wp), 1, "e4m3") @ mxq(fused, 1, "e4m3")) + f64(bp)[None, :, None]
    return y.reshape(B, C, H, W)

@@ -1,0 +1,233 @@
+from contextlib import ExitStack
+
+import concourse.mybir as mybir
+from concourse.masks import make_identity
+
+BF16 = mybir.dt.bfloat16
+F32 = mybir.dt.float32
+U32 = mybir.dt.uint32
+U8 = mybir.dt.uint8
+FP8X4 = mybir.dt.float8_e4m3fn_x4
+ALU = mybir.AluOpType
+ACT = mybir.ActivationFunctionType
+
+P = 128
+PACK = 4
+K_PASS = P * PACK
+BATCH = 2
+C = 1024
+PIXELS = 512
+GATE_PASSES = 2 * C // K_PASS
+PROJ_PASSES = C // K_PASS
+TILES = C // P
+CHUNK = 4096
+QUAD = PACK * PIXELS
+BANK_WORDS = 512
+X_VECTOR_COLS = 256
+
+FLOPS = 2 * BATCH * PIXELS * (C * 2 * C + C * C)
+
+
+def tile_crossattentionfusion_pa_kernel(tc, hsi, msi, att1, att2, wg, bg, wp, bp, out):
+    nc = tc.nc
+    with ExitStack() as ctx:
+        const = ctx.enter_context(tc.tile_pool(name="const", bufs=1))
+        keep = ctx.enter_context(tc.tile_pool(name="keep", bufs=1))
+        raw_pool = ctx.enter_context(tc.tile_pool(name="raw", bufs=8))
+        stage = ctx.enter_context(tc.tile_pool(name="stage", bufs=3))
+        gates = ctx.enter_context(tc.tile_pool(name="gates", bufs=2))
+        diffs = ctx.enter_context(tc.tile_pool(name="diffs", bufs=4))
+        results = ctx.enter_context(tc.tile_pool(name="results", bufs=4))
+        psum = ctx.enter_context(tc.psum_pool(name="psum", bufs=8))
+
+        ident = const.tile([P, P], F32)
+        make_identity(nc, ident[:])
+        bg_bf = const.tile([P, TILES], BF16)
+        nc.scalar.dma_start(out=bg_bf[:].rearrange("p (a e) -> p a e", e=2),
+                            in_=bg.rearrange("(a p e) -> p a e", p=P, e=2))
+        bp_bf = const.tile([P, TILES], BF16)
+        nc.scalar.dma_start(out=bp_bf[:], in_=bp.rearrange("(p j) -> p j", j=TILES))
+        warm = const.tile([P, 1], F32)
+        nc.vector.memset(warm[:], 0.0)
+        warm_out = const.tile([P, 1], F32)
+        nc.scalar.activation(out=warm_out[:], in_=warm[:], func=ACT.Sigmoid)
+        bg_f = const.tile([P, TILES], F32)
+        nc.vector.tensor_copy(out=bg_f[:], in_=bg_bf[:])
+        bp_f = const.tile([P, TILES], F32)
+        nc.vector.tensor_copy(out=bp_f[:], in_=bp_bf[:])
+
+        wg_codes = keep.tile([P, TILES * GATE_PASSES * P], U32, align_bytes=64)
+        wg_scales = keep.tile([P, TILES * GATE_PASSES * P], U8, align_bytes=64)
+        wp_codes = keep.tile([P, TILES * PROJ_PASSES * P], U32, align_bytes=64)
+        wp_scales = keep.tile([P, TILES * PROJ_PASSES * P], U8, align_bytes=64)
+        x_codes = keep.tile([P, BATCH * GATE_PASSES * PIXELS], U32, align_bytes=64)
+        x_scales = keep.tile([P, BATCH * GATE_PASSES * PIXELS], U8, align_bytes=64)
+        f_codes = keep.tile([P, BATCH * PROJ_PASSES * PIXELS], U32, align_bytes=64)
+        f_scales = keep.tile([P, BATCH * PROJ_PASSES * PIXELS], U8, align_bytes=64)
+
+        def load_rows(view, pieces):
+            raw = raw_pool.tile([P, CHUNK], BF16, name="raw")
+            runs = view.shape[1]
+            raw_view = raw[:].rearrange("p (a f) -> p a f", a=runs)
+            step = runs // pieces
+            for i in range(pieces):
+                nc.sync.dma_start(out=raw_view[:, i * step:(i + 1) * step, :],
+                                  in_=view[:, i * step:(i + 1) * step, :])
+            return raw
+
+        def map_view(feature_map, b):
+            return feature_map[b].rearrange("(a p e) h w -> p a (e h w)", p=P, e=2)
+
+        def prepare_weights(raw, codes, scales, vector_helps):
+            words = raw[:].bitcast(F32)
+            for half in range(2):
+                grouped = stage.tile([P, CHUNK // 2], BF16, name="w_grouped", align_bytes=64)
+                grouped_words = grouped[:].bitcast(F32)
+                for j in range(2):
+                    first = (2 * half + j) * BANK_WORDS
+                    bank = psum.tile([P, BANK_WORDS], F32, name="bank")
+                    for i in range(4):
+                        nc.tensor.transpose(bank[:, i * P:(i + 1) * P],
+                                            words[:, first + i * P:first + (i + 1) * P], ident[:])
+                    dst = grouped_words[:, j * BANK_WORDS:(j + 1) * BANK_WORDS].rearrange(
+                        "p (a c u) -> p a c u", a=2, u=2)
+                    src = bank[:].rearrange("p (a u c) -> p a c u", a=2, u=2)
+                    if vector_helps and j == 1:
+                        nc.vector.tensor_copy(out=dst, in_=src)
+                    else:
+                        nc.scalar.copy(out=dst, in_=src)
+                cols = slice(half * BANK_WORDS, (half + 1) * BANK_WORDS)
+                nc.vector.quantize_mx(out=codes[:, cols].bitcast(FP8X4), scales=scales[:, cols],
+                                      in_=grouped[:])
+
+        def prepare_x(raw, b, first_pass):
+            for g in range(2):
+                src = raw[:, g * PACK * PIXELS:(g + 1) * PACK * PIXELS].rearrange(
+                    "p (t c i) -> p c t i", t=PACK, i=4)
+                grouped = stage.tile([P, PACK * PIXELS], BF16, name="x_grouped", align_bytes=64)
+                dst = grouped[:].rearrange("p (c i t) -> p c t i", i=4, t=PACK)
+                cut = X_VECTOR_COLS // 4
+                nc.vector.tensor_copy(out=dst[:, :cut], in_=src[:, :cut])
+                nc.scalar.copy(out=dst[:, cut:], in_=src[:, cut:])
+                first = (b * GATE_PASSES + first_pass + g) * PIXELS
+                nc.vector.quantize_mx(out=x_codes[:, first:first + PIXELS].bitcast(FP8X4),
+                                      scales=x_scales[:, first:first + PIXELS], in_=grouped[:])
+
+        def load_att(b, q):
+            raw = raw_pool.tile([P, CHUNK], BF16, name="raw")
+            for i, feature_map in enumerate((att1, att2)):
+                nc.sync.dma_start(
+                    out=raw[:, i * QUAD:(i + 1) * QUAD].rearrange("p (a f) -> p a f", a=2),
+                    in_=map_view(feature_map, b)[:, 2 * q:2 * q + 2, :])
+            return raw
+
+        def difference(att_raw):
+            diff = diffs.tile([P, QUAD], F32, name="diff")
+            nc.vector.tensor_tensor(out=diff[:], in0=att_raw[:, :QUAD], in1=att_raw[:, QUAD:],
+                                    op=ALU.subtract)
+            return diff
+
+        def gate_tile(b, m, gate, diff):
+            acc = psum.tile([P, PIXELS], F32, name="bank")
+            for g in range(GATE_PASSES):
+                w_cols = slice((m * GATE_PASSES + g) * P, (m * GATE_PASSES + g + 1) * P)
+                x_cols = slice((b * GATE_PASSES + g) * PIXELS, (b * GATE_PASSES + g + 1) * PIXELS)
+                nc.tensor.matmul_mx(out=acc[:],
+                                    lhsT=wg_codes[:, w_cols].bitcast(FP8X4),
+                                    lhsT_scale=wg_scales[:, w_cols],
+                                    rhs=x_codes[:, x_cols].bitcast(FP8X4),
+                                    rhs_scale=x_scales[:, x_cols],
+                                    start=(g == 0), stop=(g == GATE_PASSES - 1))
+            cols = slice((m % PACK) * PIXELS, (m % PACK + 1) * PIXELS)
+            nc.scalar.activation(out=gate[:, cols], in_=acc[:], func=ACT.Sigmoid,
+                                 bias=bg_f[:, m:m + 1], scale=1.0)
+            nc.vector.tensor_tensor(out=gate[:, cols], in0=gate[:, cols], in1=diff[:, cols],
+                                    op=ALU.mult)
+
+        def blend(b, q, gate, att_raw):
+            fused = stage.tile([P, QUAD], BF16, name="f_grouped", align_bytes=64)
+            nc.vector.tensor_tensor(
+                out=fused[:].rearrange("p (c i t) -> p c t i", i=4, t=PACK),
+                in0=gate[:].rearrange("p (t c i) -> p c t i", t=PACK, i=4),
+                in1=att_raw[:, QUAD:].rearrange("p (t c i) -> p c t i", t=PACK, i=4),
+                op=ALU.add)
+            first = (b * PROJ_PASSES + q) * PIXELS
+            nc.vector.quantize_mx(out=f_codes[:, first:first + PIXELS].bitcast(FP8X4),
+                                  scales=f_scales[:, first:first + PIXELS], in_=fused[:])
+
+        def project(b, vector_helps):
+            out_view = out[b].rearrange("(p j) h w -> p (j h w)", j=TILES)
+            accs = [psum.tile([P, PIXELS], F32, name="bank") for j in range(TILES)]
+            for q in range(PROJ_PASSES):
+                for j in range(TILES):
+                    w_cols = slice((j * PROJ_PASSES + q) * P, (j * PROJ_PASSES + q + 1) * P)
+                    f_cols = slice((b * PROJ_PASSES + q) * PIXELS, (b * PROJ_PASSES + q + 1) * PIXELS)
+                    nc.tensor.matmul_mx(out=accs[j][:],
+                                        lhsT=wp_codes[:, w_cols].bitcast(FP8X4),
+                                        lhsT_scale=wp_scales[:, w_cols],
+                                        rhs=f_codes[:, f_cols].bitcast(FP8X4),
+                                        rhs_scale=f_scales[:, f_cols],
+                                        start=(q == 0), stop=(q == PROJ_PASSES - 1))
+            for pair in range(TILES // 2):
+                result = results.tile([P, 2 * PIXELS], F32, name="result")
+                j = 2 * pair
+                nc.scalar.activation(out=result[:, :PIXELS], in_=accs[j][:],
+                                     func=ACT.Identity, bias=bp_f[:, j:j + 1], scale=1.0)
+                if vector_helps:
+                    nc.vector.tensor_scalar(out=result[:, PIXELS:], in0=accs[j + 1][:],
+                                            scalar1=bp_f[:, j + 1:j + 2], scalar2=None, op0=ALU.add)
+                else:
+                    nc.scalar.activation(out=result[:, PIXELS:], in_=accs[j + 1][:],
+                                         func=ACT.Identity, bias=bp_f[:, j + 1:j + 2], scale=1.0)
+                nc.sync.dma_start(out=out_view[:, pair * 2 * PIXELS:(pair + 1) * 2 * PIXELS],
+                                  in_=result[:])
+
+        wg_view = wg.rearrange("(a p e) k -> p a (e k)", p=P, e=2)
+        wp_view = wp.rearrange("(p h j) k -> p h (j k)", h=2, j=TILES // 2)
+        x_raw = {}
+        x_raw[0] = [load_rows(map_view(hsi, 0), 2), load_rows(map_view(msi, 0), 2)]
+        wg_raw = [load_rows(wg_view[:, a:a + 1, :], 1) for a in range(4)]
+        x_raw[1] = [load_rows(map_view(hsi, 1), 2), load_rows(map_view(msi, 1), 2)]
+
+        def wg_chunk(a):
+            cols = slice(a * CHUNK // PACK, (a + 1) * CHUNK // PACK)
+            prepare_weights(wg_raw[a], wg_codes[:, cols], wg_scales[:, cols], True)
+
+        att_raw = {}
+        diff = {}
+        gate = {}
+        prepare_x(x_raw[0][0], 0, 0)
+        prepare_x(x_raw[0][1], 0, 2)
+        att_raw[(0, 0)] = load_att(0, 0)
+        att_raw[(0, 1)] = load_att(0, 1)
+        wg_chunk(0)
+        wg_chunk(1)
+        att_raw[(1, 0)] = load_att(1, 0)
+        att_raw[(1, 1)] = load_att(1, 1)
+        diff[(0, 0)] = difference(att_raw[(0, 0)])
+        gate[(0, 0)] = gates.tile([P, QUAD], F32, name="gate")
+        gate_tile(0, 0, gate[(0, 0)], diff[(0, 0)])
+        gate_tile(0, 1, gate[(0, 0)], diff[(0, 0)])
+        wg_chunk(2)
+        gate_tile(0, 2, gate[(0, 0)], diff[(0, 0)])
+        gate_tile(0, 3, gate[(0, 0)], diff[(0, 0)])
+        wg_chunk(3)
+        wp_raw = [load_rows(wp_view[:, h:h + 1, :], 1) for h in range(2)]
+        prepare_x(x_raw[1][0], 1, 0)
+        prepare_x(x_raw[1][1], 1, 2)
+        blend(0, 0, gate[(0, 0)], att_raw[(0, 0)])
+        diff[(0, 1)] = difference(att_raw[(0, 1)])
+        gate[(0, 1)] = gates.tile([P, QUAD], F32, name="gate")
+        for m in range(PACK, 2 * PACK):
+            gate_tile(0, m, gate[(0, 1)], diff[(0, 1)])
+        blend(0, 1, gate[(0, 1)], att_raw[(0, 1)])
+        for q in range(PROJ_PASSES):
+            diff[(1, q)] = difference(att_raw[(1, q)])
+            gate[(1, q)] = gates.tile([P, QUAD], F32, name="gate")
+            for m in range(q * PACK, (q + 1) * PACK):
+                gate_tile(1, m, gate[(1, q)], diff[(1, q)])
+            blend(1, q, gate[(1, q)], att_raw[(1, q)])
+            cols = slice(q * CHUNK // PACK, (q + 1) * CHUNK // PACK)
+            prepare_weights(wp_raw[q], wp_codes[:, cols], wp_scales[:, cols], False)
+        project(0, False)
+        project(1, True)

@@ -23,7 +23,7 @@ TILES = C // P
 CHUNK = 4096
 QUAD = PACK * PIXELS
 BANK_WORDS = 512
-X_VECTOR_COLS = 256
+X_VECTOR_COLS = (320, 128)
 
 FLOPS = 2 * BATCH * PIXELS * (C * 2 * C + C * C)
 
@@ -35,13 +35,17 @@ def tile_crossattentionfusion_pa_kernel(tc, hsi, msi, att1, att2, wg, bg, wp, bp
         keep = ctx.enter_context(tc.tile_pool(name="keep", bufs=1))
         raw_pool = ctx.enter_context(tc.tile_pool(name="raw", bufs=8))
         stage = ctx.enter_context(tc.tile_pool(name="stage", bufs=3))
-        gates = ctx.enter_context(tc.tile_pool(name="gates", bufs=2))
-        diffs = ctx.enter_context(tc.tile_pool(name="diffs", bufs=4))
+        gates = ctx.enter_context(tc.tile_pool(name="gates", bufs=3))
+        diffs = ctx.enter_context(tc.tile_pool(name="diffs", bufs=2))
         results = ctx.enter_context(tc.tile_pool(name="results", bufs=4))
         psum = ctx.enter_context(tc.psum_pool(name="psum", bufs=8))
 
         ident = const.tile([P, P], F32)
         make_identity(nc, ident[:])
+        plus = const.tile([P, P], BF16)
+        make_identity(nc, plus[:])
+        minus = const.tile([P, P], BF16)
+        nc.vector.tensor_scalar(out=minus[:], in0=plus[:], scalar1=-1.0, scalar2=None, op0=ALU.mult)
         bg_bf = const.tile([P, TILES], BF16)
         nc.scalar.dma_start(out=bg_bf[:].rearrange("p (a e) -> p a e", e=2),
                             in_=bg.rearrange("(a p e) -> p a e", p=P, e=2))
@@ -78,7 +82,7 @@ def tile_crossattentionfusion_pa_kernel(tc, hsi, msi, att1, att2, wg, bg, wp, bp
         def map_view(feature_map, b):
             return feature_map[b].rearrange("(a p e) h w -> p a (e h w)", p=P, e=2)
 
-        def prepare_weights(raw, codes, scales, vector_helps):
+        def prepare_weights(raw, codes, scales):
             words = raw[:].bitcast(F32)
             for half in range(2):
                 grouped = stage.tile([P, CHUNK // 2], BF16, name="w_grouped", align_bytes=64)
@@ -92,10 +96,7 @@ def tile_crossattentionfusion_pa_kernel(tc, hsi, msi, att1, att2, wg, bg, wp, bp
                     dst = grouped_words[:, j * BANK_WORDS:(j + 1) * BANK_WORDS].rearrange(
                         "p (a c u) -> p a c u", a=2, u=2)
                     src = bank[:].rearrange("p (a u c) -> p a c u", a=2, u=2)
-                    if vector_helps and j == 1:
-                        nc.vector.tensor_copy(out=dst, in_=src)
-                    else:
-                        nc.scalar.copy(out=dst, in_=src)
+                    nc.scalar.copy(out=dst, in_=src)
                 cols = slice(half * BANK_WORDS, (half + 1) * BANK_WORDS)
                 nc.vector.quantize_mx(out=codes[:, cols].bitcast(FP8X4), scales=scales[:, cols],
                                       in_=grouped[:])
@@ -106,7 +107,7 @@ def tile_crossattentionfusion_pa_kernel(tc, hsi, msi, att1, att2, wg, bg, wp, bp
                     "p (t c i) -> p c t i", t=PACK, i=4)
                 grouped = stage.tile([P, PACK * PIXELS], BF16, name="x_grouped", align_bytes=64)
                 dst = grouped[:].rearrange("p (c i t) -> p c t i", i=4, t=PACK)
-                cut = X_VECTOR_COLS // 4
+                cut = X_VECTOR_COLS[b] // 4
                 nc.vector.tensor_copy(out=dst[:, :cut], in_=src[:, :cut])
                 nc.scalar.copy(out=dst[:, cut:], in_=src[:, cut:])
                 first = (b * GATE_PASSES + first_pass + g) * PIXELS
@@ -127,7 +128,7 @@ def tile_crossattentionfusion_pa_kernel(tc, hsi, msi, att1, att2, wg, bg, wp, bp
                                     op=ALU.subtract)
             return diff
 
-        def gate_tile(b, m, gate, diff):
+        def gate_tile(b, m, gate, diff, att_tile):
             acc = psum.tile([P, PIXELS], F32, name="bank")
             for g in range(GATE_PASSES):
                 w_cols = slice((m * GATE_PASSES + g) * P, (m * GATE_PASSES + g + 1) * P)
@@ -138,10 +139,21 @@ def tile_crossattentionfusion_pa_kernel(tc, hsi, msi, att1, att2, wg, bg, wp, bp
                                     rhs=x_codes[:, x_cols].bitcast(FP8X4),
                                     rhs_scale=x_scales[:, x_cols],
                                     start=(g == 0), stop=(g == GATE_PASSES - 1))
-            cols = slice((m % PACK) * PIXELS, (m % PACK + 1) * PIXELS)
+            first = (m % PACK) * PIXELS
+            cols = slice(first, first + PIXELS)
+            if diff is None:
+                diff_bank = psum.tile([P, PIXELS], F32, name="bank")
+                nc.tensor.matmul(out=diff_bank[:], lhsT=plus[:], rhs=att_tile[:, cols],
+                                 start=True, stop=False)
+                nc.tensor.matmul(out=diff_bank[:], lhsT=minus[:],
+                                 rhs=att_tile[:, QUAD + first:QUAD + first + PIXELS],
+                                 start=False, stop=True)
+                difference_of_tile = diff_bank[:]
+            else:
+                difference_of_tile = diff[:, cols]
             nc.scalar.activation(out=gate[:, cols], in_=acc[:], func=ACT.Sigmoid,
                                  bias=bg_f[:, m:m + 1], scale=1.0)
-            nc.vector.tensor_tensor(out=gate[:, cols], in0=gate[:, cols], in1=diff[:, cols],
+            nc.vector.tensor_tensor(out=gate[:, cols], in0=gate[:, cols], in1=difference_of_tile,
                                     op=ALU.mult)
 
         def blend(b, q, gate, att_raw):
@@ -157,77 +169,91 @@ def tile_crossattentionfusion_pa_kernel(tc, hsi, msi, att1, att2, wg, bg, wp, bp
 
         def project(b, vector_helps):
             out_view = out[b].rearrange("(p j) h w -> p (j h w)", j=TILES)
-            accs = [psum.tile([P, PIXELS], F32, name="bank") for j in range(TILES)]
-            for q in range(PROJ_PASSES):
-                for j in range(TILES):
-                    w_cols = slice((j * PROJ_PASSES + q) * P, (j * PROJ_PASSES + q + 1) * P)
-                    f_cols = slice((b * PROJ_PASSES + q) * PIXELS, (b * PROJ_PASSES + q + 1) * PIXELS)
-                    nc.tensor.matmul_mx(out=accs[j][:],
-                                        lhsT=wp_codes[:, w_cols].bitcast(FP8X4),
-                                        lhsT_scale=wp_scales[:, w_cols],
-                                        rhs=f_codes[:, f_cols].bitcast(FP8X4),
-                                        rhs_scale=f_scales[:, f_cols],
-                                        start=(q == 0), stop=(q == PROJ_PASSES - 1))
             for pair in range(TILES // 2):
                 result = results.tile([P, 2 * PIXELS], F32, name="result")
-                j = 2 * pair
-                nc.scalar.activation(out=result[:, :PIXELS], in_=accs[j][:],
-                                     func=ACT.Identity, bias=bp_f[:, j:j + 1], scale=1.0)
-                if vector_helps:
-                    nc.vector.tensor_scalar(out=result[:, PIXELS:], in0=accs[j + 1][:],
-                                            scalar1=bp_f[:, j + 1:j + 2], scalar2=None, op0=ALU.add)
-                else:
-                    nc.scalar.activation(out=result[:, PIXELS:], in_=accs[j + 1][:],
-                                         func=ACT.Identity, bias=bp_f[:, j + 1:j + 2], scale=1.0)
+                for i in range(2):
+                    j = 2 * pair + i
+                    acc = psum.tile([P, PIXELS], F32, name="bank")
+                    for q in range(PROJ_PASSES):
+                        w_cols = slice((j * PROJ_PASSES + q) * P, (j * PROJ_PASSES + q + 1) * P)
+                        f_cols = slice((b * PROJ_PASSES + q) * PIXELS, (b * PROJ_PASSES + q + 1) * PIXELS)
+                        nc.tensor.matmul_mx(out=acc[:],
+                                            lhsT=wp_codes[:, w_cols].bitcast(FP8X4),
+                                            lhsT_scale=wp_scales[:, w_cols],
+                                            rhs=f_codes[:, f_cols].bitcast(FP8X4),
+                                            rhs_scale=f_scales[:, f_cols],
+                                            start=(q == 0), stop=(q == PROJ_PASSES - 1))
+                    cols = slice(i * PIXELS, (i + 1) * PIXELS)
+                    if vector_helps and i == 1:
+                        nc.vector.tensor_scalar(out=result[:, cols], in0=acc[:],
+                                                scalar1=bp_f[:, j:j + 1], scalar2=None, op0=ALU.add)
+                    else:
+                        nc.scalar.activation(out=result[:, cols], in_=acc[:], func=ACT.Identity,
+                                             bias=bp_f[:, j:j + 1], scale=1.0)
                 nc.sync.dma_start(out=out_view[:, pair * 2 * PIXELS:(pair + 1) * 2 * PIXELS],
                                   in_=result[:])
 
         wg_view = wg.rearrange("(a p e) k -> p a (e k)", p=P, e=2)
         wp_view = wp.rearrange("(p h j) k -> p h (j k)", h=2, j=TILES // 2)
         x_raw = {}
-        x_raw[0] = [load_rows(map_view(hsi, 0), 2), load_rows(map_view(msi, 0), 2)]
-        wg_raw = [load_rows(wg_view[:, a:a + 1, :], 1) for a in range(4)]
-        x_raw[1] = [load_rows(map_view(hsi, 1), 2), load_rows(map_view(msi, 1), 2)]
-
-        def wg_chunk(a):
-            cols = slice(a * CHUNK // PACK, (a + 1) * CHUNK // PACK)
-            prepare_weights(wg_raw[a], wg_codes[:, cols], wg_scales[:, cols], True)
-
+        wg_raw = {}
+        wp_raw = {}
         att_raw = {}
         diff = {}
         gate = {}
-        prepare_x(x_raw[0][0], 0, 0)
-        prepare_x(x_raw[0][1], 0, 2)
+
+        def wg_chunk(a):
+            cols = slice(a * CHUNK // PACK, (a + 1) * CHUNK // PACK)
+            prepare_weights(wg_raw[a], wg_codes[:, cols], wg_scales[:, cols])
+
+        def wp_chunk(h):
+            cols = slice(h * CHUNK // PACK, (h + 1) * CHUNK // PACK)
+            prepare_weights(wp_raw[h], wp_codes[:, cols], wp_scales[:, cols])
+
+        def start_quad(b, q):
+            diff[(b, q)] = difference(att_raw[(b, q)]) if q == 0 else None
+            gate[(b, q)] = gates.tile([P, QUAD], F32, name="gate")
+
+        def gate_tiles(b, tiles):
+            for m in tiles:
+                gate_tile(b, m, gate[(b, m // PACK)], diff[(b, m // PACK)], att_raw[(b, m // PACK)])
+
+        x_raw[(0, 0)] = load_rows(map_view(hsi, 0), 2)
+        x_raw[(0, 1)] = load_rows(map_view(msi, 0), 2)
+        wg_raw[0] = load_rows(wg_view[:, 0:1, :], 1)
+        wg_raw[1] = load_rows(wg_view[:, 1:2, :], 1)
         att_raw[(0, 0)] = load_att(0, 0)
+        wg_raw[2] = load_rows(wg_view[:, 2:3, :], 1)
+        wg_raw[3] = load_rows(wg_view[:, 3:4, :], 1)
+        x_raw[(1, 0)] = load_rows(map_view(hsi, 1), 2)
+        prepare_x(x_raw[(0, 0)], 0, 0)
+        x_raw[(1, 1)] = load_rows(map_view(msi, 1), 2)
+        prepare_x(x_raw[(0, 1)], 0, 2)
         att_raw[(0, 1)] = load_att(0, 1)
         wg_chunk(0)
-        wg_chunk(1)
         att_raw[(1, 0)] = load_att(1, 0)
+        wg_chunk(1)
         att_raw[(1, 1)] = load_att(1, 1)
-        diff[(0, 0)] = difference(att_raw[(0, 0)])
-        gate[(0, 0)] = gates.tile([P, QUAD], F32, name="gate")
-        gate_tile(0, 0, gate[(0, 0)], diff[(0, 0)])
-        gate_tile(0, 1, gate[(0, 0)], diff[(0, 0)])
+        start_quad(0, 0)
+        gate_tiles(0, (0, 1))
         wg_chunk(2)
-        gate_tile(0, 2, gate[(0, 0)], diff[(0, 0)])
-        gate_tile(0, 3, gate[(0, 0)], diff[(0, 0)])
+        wp_raw[0] = load_rows(wp_view[:, 0:1, :], 1)
+        gate_tiles(0, (2, 3))
         wg_chunk(3)
-        wp_raw = [load_rows(wp_view[:, h:h + 1, :], 1) for h in range(2)]
-        prepare_x(x_raw[1][0], 1, 0)
-        prepare_x(x_raw[1][1], 1, 2)
+        wp_raw[1] = load_rows(wp_view[:, 1:2, :], 1)
         blend(0, 0, gate[(0, 0)], att_raw[(0, 0)])
-        diff[(0, 1)] = difference(att_raw[(0, 1)])
-        gate[(0, 1)] = gates.tile([P, QUAD], F32, name="gate")
-        for m in range(PACK, 2 * PACK):
-            gate_tile(0, m, gate[(0, 1)], diff[(0, 1)])
+        prepare_x(x_raw[(1, 0)], 1, 0)
+        prepare_x(x_raw[(1, 1)], 1, 2)
+        start_quad(0, 1)
+        gate_tiles(0, (4, 5, 6, 7))
         blend(0, 1, gate[(0, 1)], att_raw[(0, 1)])
-        for q in range(PROJ_PASSES):
-            diff[(1, q)] = difference(att_raw[(1, q)])
-            gate[(1, q)] = gates.tile([P, QUAD], F32, name="gate")
-            for m in range(q * PACK, (q + 1) * PACK):
-                gate_tile(1, m, gate[(1, q)], diff[(1, q)])
-            blend(1, q, gate[(1, q)], att_raw[(1, q)])
-            cols = slice(q * CHUNK // PACK, (q + 1) * CHUNK // PACK)
-            prepare_weights(wp_raw[q], wp_codes[:, cols], wp_scales[:, cols], False)
+        start_quad(1, 0)
+        gate_tiles(1, (0, 1, 2, 3))
+        wp_chunk(0)
+        wp_chunk(1)
+        blend(1, 0, gate[(1, 0)], att_raw[(1, 0)])
+        start_quad(1, 1)
+        gate_tiles(1, (4, 5, 6, 7))
         project(0, False)
+        blend(1, 1, gate[(1, 1)], att_raw[(1, 1)])
         project(1, True)

@@ -36,7 +36,6 @@ def tile_crossattentionfusion_pa_kernel(tc, hsi, msi, att1, att2, wg, bg, wp, bp
         raw_pool = ctx.enter_context(tc.tile_pool(name="raw", bufs=8))
         stage = ctx.enter_context(tc.tile_pool(name="stage", bufs=3))
         gates = ctx.enter_context(tc.tile_pool(name="gates", bufs=3))
-        diffs = ctx.enter_context(tc.tile_pool(name="diffs", bufs=2))
         results = ctx.enter_context(tc.tile_pool(name="results", bufs=4))
         psum = ctx.enter_context(tc.psum_pool(name="psum", bufs=8))
 
@@ -122,13 +121,7 @@ def tile_crossattentionfusion_pa_kernel(tc, hsi, msi, att1, att2, wg, bg, wp, bp
                     in_=map_view(feature_map, b)[:, 2 * q:2 * q + 2, :])
             return raw
 
-        def difference(att_raw):
-            diff = diffs.tile([P, QUAD], F32, name="diff")
-            nc.vector.tensor_tensor(out=diff[:], in0=att_raw[:, :QUAD], in1=att_raw[:, QUAD:],
-                                    op=ALU.subtract)
-            return diff
-
-        def gate_tile(b, m, gate, diff, att_tile):
+        def gate_tile(b, m, gate, att_tile):
             acc = psum.tile([P, PIXELS], F32, name="bank")
             for g in range(GATE_PASSES):
                 w_cols = slice((m * GATE_PASSES + g) * P, (m * GATE_PASSES + g + 1) * P)
@@ -141,19 +134,15 @@ def tile_crossattentionfusion_pa_kernel(tc, hsi, msi, att1, att2, wg, bg, wp, bp
                                     start=(g == 0), stop=(g == GATE_PASSES - 1))
             first = (m % PACK) * PIXELS
             cols = slice(first, first + PIXELS)
-            if diff is None:
-                diff_bank = psum.tile([P, PIXELS], F32, name="bank")
-                nc.tensor.matmul(out=diff_bank[:], lhsT=plus[:], rhs=att_tile[:, cols],
-                                 start=True, stop=False)
-                nc.tensor.matmul(out=diff_bank[:], lhsT=minus[:],
-                                 rhs=att_tile[:, QUAD + first:QUAD + first + PIXELS],
-                                 start=False, stop=True)
-                difference_of_tile = diff_bank[:]
-            else:
-                difference_of_tile = diff[:, cols]
+            diff_bank = psum.tile([P, PIXELS], F32, name="bank")
+            nc.tensor.matmul(out=diff_bank[:], lhsT=plus[:], rhs=att_tile[:, cols],
+                             start=True, stop=False)
+            nc.tensor.matmul(out=diff_bank[:], lhsT=minus[:],
+                             rhs=att_tile[:, QUAD + first:QUAD + first + PIXELS],
+                             start=False, stop=True)
             nc.scalar.activation(out=gate[:, cols], in_=acc[:], func=ACT.Sigmoid,
                                  bias=bg_f[:, m:m + 1], scale=1.0)
-            nc.vector.tensor_tensor(out=gate[:, cols], in0=gate[:, cols], in1=difference_of_tile,
+            nc.vector.tensor_tensor(out=gate[:, cols], in0=gate[:, cols], in1=diff_bank[:],
                                     op=ALU.mult)
 
         def blend(b, q, gate, att_raw):
@@ -199,7 +188,6 @@ def tile_crossattentionfusion_pa_kernel(tc, hsi, msi, att1, att2, wg, bg, wp, bp
         wg_raw = {}
         wp_raw = {}
         att_raw = {}
-        diff = {}
         gate = {}
 
         def wg_chunk(a):
@@ -211,12 +199,11 @@ def tile_crossattentionfusion_pa_kernel(tc, hsi, msi, att1, att2, wg, bg, wp, bp
             prepare_weights(wp_raw[h], wp_codes[:, cols], wp_scales[:, cols])
 
         def start_quad(b, q):
-            diff[(b, q)] = difference(att_raw[(b, q)]) if q == 0 else None
             gate[(b, q)] = gates.tile([P, QUAD], F32, name="gate")
 
         def gate_tiles(b, tiles):
             for m in tiles:
-                gate_tile(b, m, gate[(b, m // PACK)], diff[(b, m // PACK)], att_raw[(b, m // PACK)])
+                gate_tile(b, m, gate[(b, m // PACK)], att_raw[(b, m // PACK)])
 
         x_raw[(0, 0)] = load_rows(map_view(hsi, 0), 2)
         x_raw[(0, 1)] = load_rows(map_view(msi, 0), 2)

@@ -20,10 +20,20 @@ PIXELS = 512
 GATE_PASSES = 2 * C // K_PASS
 PROJ_PASSES = C // K_PASS
 TILES = C // P
-CHUNK = 4096
-QUAD = PACK * PIXELS
+GROUP = PACK * PIXELS
+CHUNK = 2 * GROUP
 BANK_WORDS = 512
-X_VECTOR_COLS = (320, 128)
+PAIR = 2
+RUN = 4
+
+X_VECTOR_PIXELS = (320, 128)
+
+RAW_BUFS = 8
+STAGE_BUFS = 3
+GATE_BUFS = 3
+DIFF_BUFS = 2
+RESULT_BUFS = 4
+PSUM_BANKS = 8
 
 FLOPS = 2 * BATCH * PIXELS * (C * 2 * C + C * C)
 
@@ -33,11 +43,12 @@ def tile_crossattentionfusion_pa_kernel(tc, hsi, msi, att1, att2, wg, bg, wp, bp
     with ExitStack() as ctx:
         const = ctx.enter_context(tc.tile_pool(name="const", bufs=1))
         keep = ctx.enter_context(tc.tile_pool(name="keep", bufs=1))
-        raw_pool = ctx.enter_context(tc.tile_pool(name="raw", bufs=8))
-        stage = ctx.enter_context(tc.tile_pool(name="stage", bufs=3))
-        gates = ctx.enter_context(tc.tile_pool(name="gates", bufs=3))
-        results = ctx.enter_context(tc.tile_pool(name="results", bufs=4))
-        psum = ctx.enter_context(tc.psum_pool(name="psum", bufs=8))
+        raw_pool = ctx.enter_context(tc.tile_pool(name="raw", bufs=RAW_BUFS))
+        stage = ctx.enter_context(tc.tile_pool(name="stage", bufs=STAGE_BUFS))
+        gates = ctx.enter_context(tc.tile_pool(name="gates", bufs=GATE_BUFS))
+        diffs = ctx.enter_context(tc.tile_pool(name="diffs", bufs=DIFF_BUFS))
+        results = ctx.enter_context(tc.tile_pool(name="results", bufs=RESULT_BUFS))
+        psum = ctx.enter_context(tc.psum_pool(name="psum", bufs=PSUM_BANKS))
 
         ident = const.tile([P, P], F32)
         make_identity(nc, ident[:])
@@ -46,8 +57,8 @@ def tile_crossattentionfusion_pa_kernel(tc, hsi, msi, att1, att2, wg, bg, wp, bp
         minus = const.tile([P, P], BF16)
         nc.vector.tensor_scalar(out=minus[:], in0=plus[:], scalar1=-1.0, scalar2=None, op0=ALU.mult)
         bg_bf = const.tile([P, TILES], BF16)
-        nc.scalar.dma_start(out=bg_bf[:].rearrange("p (a e) -> p a e", e=2),
-                            in_=bg.rearrange("(a p e) -> p a e", p=P, e=2))
+        nc.scalar.dma_start(out=bg_bf[:].rearrange("p (a e) -> p a e", e=PAIR),
+                            in_=bg.rearrange("(a p e) -> p a e", p=P, e=PAIR))
         bp_bf = const.tile([P, TILES], BF16)
         nc.scalar.dma_start(out=bp_bf[:], in_=bp.rearrange("(p j) -> p j", j=TILES))
         warm = const.tile([P, 1], F32)
@@ -79,7 +90,18 @@ def tile_crossattentionfusion_pa_kernel(tc, hsi, msi, att1, att2, wg, bg, wp, bp
             return raw
 
         def map_view(feature_map, b):
-            return feature_map[b].rearrange("(a p e) h w -> p a (e h w)", p=P, e=2)
+            return feature_map[b].rearrange("(a p e) h w -> p a (e h w)", p=P, e=PAIR)
+
+        def load_x(feature_map, b):
+            return load_rows(map_view(feature_map, b), 2)
+
+        def load_att(b, q):
+            raw = raw_pool.tile([P, CHUNK], BF16, name="raw")
+            for i, feature_map in enumerate((att1, att2)):
+                nc.sync.dma_start(
+                    out=raw[:, i * GROUP:(i + 1) * GROUP].rearrange("p (a f) -> p a f", a=PAIR),
+                    in_=map_view(feature_map, b)[:, PAIR * q:PAIR * q + PAIR, :])
+            return raw
 
         def prepare_weights(raw, codes, scales):
             words = raw[:].bitcast(F32)
@@ -89,39 +111,39 @@ def tile_crossattentionfusion_pa_kernel(tc, hsi, msi, att1, att2, wg, bg, wp, bp
                 for j in range(2):
                     first = (2 * half + j) * BANK_WORDS
                     bank = psum.tile([P, BANK_WORDS], F32, name="bank")
-                    for i in range(4):
+                    for i in range(BANK_WORDS // P):
                         nc.tensor.transpose(bank[:, i * P:(i + 1) * P],
                                             words[:, first + i * P:first + (i + 1) * P], ident[:])
                     dst = grouped_words[:, j * BANK_WORDS:(j + 1) * BANK_WORDS].rearrange(
-                        "p (a c u) -> p a c u", a=2, u=2)
-                    src = bank[:].rearrange("p (a u c) -> p a c u", a=2, u=2)
+                        "p (a c u) -> p a c u", a=2, u=PAIR)
+                    src = bank[:].rearrange("p (a u c) -> p a c u", a=2, u=PAIR)
                     nc.scalar.copy(out=dst, in_=src)
                 cols = slice(half * BANK_WORDS, (half + 1) * BANK_WORDS)
                 nc.vector.quantize_mx(out=codes[:, cols].bitcast(FP8X4), scales=scales[:, cols],
                                       in_=grouped[:])
 
         def prepare_x(raw, b, first_pass):
+            grouped = []
             for g in range(2):
-                src = raw[:, g * PACK * PIXELS:(g + 1) * PACK * PIXELS].rearrange(
-                    "p (t c i) -> p c t i", t=PACK, i=4)
-                grouped = stage.tile([P, PACK * PIXELS], BF16, name="x_grouped", align_bytes=64)
-                dst = grouped[:].rearrange("p (c i t) -> p c t i", i=4, t=PACK)
-                cut = X_VECTOR_COLS[b] // 4
+                src = raw[:, g * GROUP:(g + 1) * GROUP].rearrange(
+                    "p (t c i) -> p c t i", t=PACK, i=RUN)
+                grouped.append(stage.tile([P, GROUP], BF16, name="x_grouped", align_bytes=64))
+                dst = grouped[g][:].rearrange("p (c i t) -> p c t i", i=RUN, t=PACK)
+                cut = X_VECTOR_PIXELS[b] // RUN
                 nc.vector.tensor_copy(out=dst[:, :cut], in_=src[:, :cut])
                 nc.scalar.copy(out=dst[:, cut:], in_=src[:, cut:])
+            for g in range(2):
                 first = (b * GATE_PASSES + first_pass + g) * PIXELS
                 nc.vector.quantize_mx(out=x_codes[:, first:first + PIXELS].bitcast(FP8X4),
-                                      scales=x_scales[:, first:first + PIXELS], in_=grouped[:])
+                                      scales=x_scales[:, first:first + PIXELS], in_=grouped[g][:])
 
-        def load_att(b, q):
-            raw = raw_pool.tile([P, CHUNK], BF16, name="raw")
-            for i, feature_map in enumerate((att1, att2)):
-                nc.sync.dma_start(
-                    out=raw[:, i * QUAD:(i + 1) * QUAD].rearrange("p (a f) -> p a f", a=2),
-                    in_=map_view(feature_map, b)[:, 2 * q:2 * q + 2, :])
-            return raw
+        def difference(att_raw):
+            diff = diffs.tile([P, GROUP], F32, name="diff")
+            nc.vector.tensor_tensor(out=diff[:], in0=att_raw[:, :GROUP], in1=att_raw[:, GROUP:],
+                                    op=ALU.subtract)
+            return diff
 
-        def gate_tile(b, m, gate, att_tile):
+        def gate_tile(b, m, gate, diff, att_raw):
             acc = psum.tile([P, PIXELS], F32, name="bank")
             for g in range(GATE_PASSES):
                 w_cols = slice((m * GATE_PASSES + g) * P, (m * GATE_PASSES + g + 1) * P)
@@ -134,27 +156,36 @@ def tile_crossattentionfusion_pa_kernel(tc, hsi, msi, att1, att2, wg, bg, wp, bp
                                     start=(g == 0), stop=(g == GATE_PASSES - 1))
             first = (m % PACK) * PIXELS
             cols = slice(first, first + PIXELS)
-            diff_bank = psum.tile([P, PIXELS], F32, name="bank")
-            nc.tensor.matmul(out=diff_bank[:], lhsT=plus[:], rhs=att_tile[:, cols],
-                             start=True, stop=False)
-            nc.tensor.matmul(out=diff_bank[:], lhsT=minus[:],
-                             rhs=att_tile[:, QUAD + first:QUAD + first + PIXELS],
-                             start=False, stop=True)
+            if diff is None:
+                diff_bank = psum.tile([P, PIXELS], F32, name="bank")
+                nc.tensor.matmul(out=diff_bank[:], lhsT=plus[:], rhs=att_raw[:, cols],
+                                 start=True, stop=False)
+                nc.tensor.matmul(out=diff_bank[:], lhsT=minus[:],
+                                 rhs=att_raw[:, GROUP + first:GROUP + first + PIXELS],
+                                 start=False, stop=True)
+                difference_of_tile = diff_bank[:]
+            else:
+                difference_of_tile = diff[:, cols]
             nc.scalar.activation(out=gate[:, cols], in_=acc[:], func=ACT.Sigmoid,
                                  bias=bg_f[:, m:m + 1], scale=1.0)
-            nc.vector.tensor_tensor(out=gate[:, cols], in0=gate[:, cols], in1=diff_bank[:],
+            nc.vector.tensor_tensor(out=gate[:, cols], in0=gate[:, cols], in1=difference_of_tile,
                                     op=ALU.mult)
 
         def blend(b, q, gate, att_raw):
-            fused = stage.tile([P, QUAD], BF16, name="f_grouped", align_bytes=64)
-            nc.vector.tensor_tensor(
-                out=fused[:].rearrange("p (c i t) -> p c t i", i=4, t=PACK),
-                in0=gate[:].rearrange("p (t c i) -> p c t i", t=PACK, i=4),
-                in1=att_raw[:, QUAD:].rearrange("p (t c i) -> p c t i", t=PACK, i=4),
-                op=ALU.add)
-            first = (b * PROJ_PASSES + q) * PIXELS
-            nc.vector.quantize_mx(out=f_codes[:, first:first + PIXELS].bitcast(FP8X4),
-                                  scales=f_scales[:, first:first + PIXELS], in_=fused[:])
+            fused = stage.tile([P, GROUP], BF16, name="f_grouped", align_bytes=64)
+            fused_view = fused[:].rearrange("p (c i t) -> p c t i", i=RUN, t=PACK)
+            gate_view = gate[:].rearrange("p (t c i) -> p c t i", t=PACK, i=RUN)
+            att2_view = att_raw[:, GROUP:].rearrange("p (t c i) -> p c t i", t=PACK, i=RUN)
+            runs = PIXELS // RUN // 2
+            for h in range(2):
+                part = slice(h * runs, (h + 1) * runs)
+                nc.vector.tensor_tensor(out=fused_view[:, part], in0=gate_view[:, part],
+                                        in1=att2_view[:, part], op=ALU.add)
+            for h in range(2):
+                first = (b * PROJ_PASSES + q) * PIXELS + h * PIXELS // 2
+                cols = slice(first, first + PIXELS // 2)
+                nc.vector.quantize_mx(out=f_codes[:, cols].bitcast(FP8X4), scales=f_scales[:, cols],
+                                      in_=fused[:, h * GROUP // 2:(h + 1) * GROUP // 2])
 
         def project(b, vector_helps):
             out_view = out[b].rearrange("(p j) h w -> p (j h w)", j=TILES)
@@ -165,7 +196,8 @@ def tile_crossattentionfusion_pa_kernel(tc, hsi, msi, att1, att2, wg, bg, wp, bp
                     acc = psum.tile([P, PIXELS], F32, name="bank")
                     for q in range(PROJ_PASSES):
                         w_cols = slice((j * PROJ_PASSES + q) * P, (j * PROJ_PASSES + q + 1) * P)
-                        f_cols = slice((b * PROJ_PASSES + q) * PIXELS, (b * PROJ_PASSES + q + 1) * PIXELS)
+                        f_cols = slice((b * PROJ_PASSES + q) * PIXELS,
+                                       (b * PROJ_PASSES + q + 1) * PIXELS)
                         nc.tensor.matmul_mx(out=acc[:],
                                             lhsT=wp_codes[:, w_cols].bitcast(FP8X4),
                                             lhsT_scale=wp_scales[:, w_cols],
@@ -182,12 +214,13 @@ def tile_crossattentionfusion_pa_kernel(tc, hsi, msi, att1, att2, wg, bg, wp, bp
                 nc.sync.dma_start(out=out_view[:, pair * 2 * PIXELS:(pair + 1) * 2 * PIXELS],
                                   in_=result[:])
 
-        wg_view = wg.rearrange("(a p e) k -> p a (e k)", p=P, e=2)
+        wg_view = wg.rearrange("(a p e) k -> p a (e k)", p=P, e=PAIR)
         wp_view = wp.rearrange("(p h j) k -> p h (j k)", h=2, j=TILES // 2)
         x_raw = {}
         wg_raw = {}
         wp_raw = {}
         att_raw = {}
+        diff = {}
         gate = {}
 
         def wg_chunk(a):
@@ -198,30 +231,33 @@ def tile_crossattentionfusion_pa_kernel(tc, hsi, msi, att1, att2, wg, bg, wp, bp
             cols = slice(h * CHUNK // PACK, (h + 1) * CHUNK // PACK)
             prepare_weights(wp_raw[h], wp_codes[:, cols], wp_scales[:, cols])
 
-        def start_quad(b, q):
-            gate[(b, q)] = gates.tile([P, QUAD], F32, name="gate")
+        def start_group(b, q):
+            diff[(b, q)] = difference(att_raw[(b, q)]) if q == 0 else None
+            gate[(b, q)] = gates.tile([P, GROUP], F32, name="gate")
 
         def gate_tiles(b, tiles):
             for m in tiles:
-                gate_tile(b, m, gate[(b, m // PACK)], att_raw[(b, m // PACK)])
+                q = m // PACK
+                gate_tile(b, m, gate[(b, q)], diff[(b, q)], att_raw[(b, q)])
 
-        x_raw[(0, 0)] = load_rows(map_view(hsi, 0), 2)
-        x_raw[(0, 1)] = load_rows(map_view(msi, 0), 2)
+        x_raw[(0, 0)] = load_x(hsi, 0)
+        x_raw[(0, 1)] = load_x(msi, 0)
         wg_raw[0] = load_rows(wg_view[:, 0:1, :], 1)
         wg_raw[1] = load_rows(wg_view[:, 1:2, :], 1)
         att_raw[(0, 0)] = load_att(0, 0)
         wg_raw[2] = load_rows(wg_view[:, 2:3, :], 1)
         wg_raw[3] = load_rows(wg_view[:, 3:4, :], 1)
-        x_raw[(1, 0)] = load_rows(map_view(hsi, 1), 2)
+        x_raw[(1, 0)] = load_x(hsi, 1)
+
         prepare_x(x_raw[(0, 0)], 0, 0)
-        x_raw[(1, 1)] = load_rows(map_view(msi, 1), 2)
+        x_raw[(1, 1)] = load_x(msi, 1)
         prepare_x(x_raw[(0, 1)], 0, 2)
         att_raw[(0, 1)] = load_att(0, 1)
         wg_chunk(0)
         att_raw[(1, 0)] = load_att(1, 0)
         wg_chunk(1)
         att_raw[(1, 1)] = load_att(1, 1)
-        start_quad(0, 0)
+        start_group(0, 0)
         gate_tiles(0, (0, 1))
         wg_chunk(2)
         wp_raw[0] = load_rows(wp_view[:, 0:1, :], 1)
@@ -231,15 +267,16 @@ def tile_crossattentionfusion_pa_kernel(tc, hsi, msi, att1, att2, wg, bg, wp, bp
         blend(0, 0, gate[(0, 0)], att_raw[(0, 0)])
         prepare_x(x_raw[(1, 0)], 1, 0)
         prepare_x(x_raw[(1, 1)], 1, 2)
-        start_quad(0, 1)
+        start_group(0, 1)
         gate_tiles(0, (4, 5, 6, 7))
         blend(0, 1, gate[(0, 1)], att_raw[(0, 1)])
-        start_quad(1, 0)
+
+        start_group(1, 0)
         gate_tiles(1, (0, 1, 2, 3))
         wp_chunk(0)
         wp_chunk(1)
         blend(1, 0, gate[(1, 0)], att_raw[(1, 0)])
-        start_quad(1, 1)
+        start_group(1, 1)
         gate_tiles(1, (4, 5, 6, 7))
         project(0, False)
         blend(1, 1, gate[(1, 1)], att_raw[(1, 1)])

@@ -56,11 +56,15 @@ def tile_crossattentionfusion_pa_kernel(tc, hsi, msi, att1, att2, wg, bg, wp, bp
         make_identity(nc, plus[:])
         minus = const.tile([P, P], BF16)
         nc.vector.tensor_scalar(out=minus[:], in0=plus[:], scalar1=-1.0, scalar2=None, op0=ALU.mult)
+        bg_rows = const.tile([P, P], F32)
+        nc.vector.memset(bg_rows[:], 0.0)
+        nc.scalar.dma_start(out=bg_rows[0:TILES // PAIR, :].bitcast(BF16),
+                            in_=bg.rearrange("(a w) -> a w", a=TILES // PAIR))
+        bg_bank = psum.tile([P, P], F32, name="bank")
+        nc.tensor.transpose(bg_bank[:], bg_rows[:], ident[:])
         bg_bf = const.tile([P, TILES], BF16)
-        nc.scalar.dma_start(out=bg_bf[:].rearrange("p (a e) -> p a e", e=PAIR),
-                            in_=bg.rearrange("(a p e) -> p a e", p=P, e=PAIR))
+        nc.vector.tensor_copy(out=bg_bf[:].bitcast(F32), in_=bg_bank[:, 0:TILES // PAIR])
         bp_bf = const.tile([P, TILES], BF16)
-        nc.scalar.dma_start(out=bp_bf[:], in_=bp.rearrange("(p j) -> p j", j=TILES))
         warm = const.tile([P, 1], F32)
         nc.vector.memset(warm[:], 0.0)
         warm_out = const.tile([P, 1], F32)
@@ -68,7 +72,6 @@ def tile_crossattentionfusion_pa_kernel(tc, hsi, msi, att1, att2, wg, bg, wp, bp
         bg_f = const.tile([P, TILES], F32)
         nc.vector.tensor_copy(out=bg_f[:], in_=bg_bf[:])
         bp_f = const.tile([P, TILES], F32)
-        nc.vector.tensor_copy(out=bp_f[:], in_=bp_bf[:])
 
         wg_codes = keep.tile([P, TILES * GATE_PASSES * P], U32, align_bytes=64)
         wg_scales = keep.tile([P, TILES * GATE_PASSES * P], U8, align_bytes=64)
@@ -264,6 +267,8 @@ def tile_crossattentionfusion_pa_kernel(tc, hsi, msi, att1, att2, wg, bg, wp, bp
         gate_tiles(0, (2, 3))
         wg_chunk(3)
         wp_raw[1] = load_rows(wp_view[:, 1:2, :], 1)
+        nc.sync.dma_start(out=bp_bf[:], in_=bp.rearrange("(p j) -> p j", j=TILES))
+        nc.vector.tensor_copy(out=bp_f[:], in_=bp_bf[:])
         blend(0, 0, gate[(0, 0)], att_raw[(0, 0)])
         prepare_x(x_raw[(1, 0)], 1, 0)
         prepare_x(x_raw[(1, 1)], 1, 2)

@@ -95,8 +95,8 @@ def tile_crossattentionfusion_pa_kernel(tc, hsi, msi, att1, att2, wg, bg, wp, bp
         def map_view(feature_map, b):
             return feature_map[b].rearrange("(a p e) h w -> p a (e h w)", p=P, e=PAIR)
 
-        def load_x(feature_map, b):
-            return load_rows(map_view(feature_map, b), 2)
+        def load_x(feature_map, b, pieces):
+            return load_rows(map_view(feature_map, b), pieces)
 
         def load_att(b, q):
             raw = raw_pool.tile([P, CHUNK], BF16, name="raw")
@@ -243,17 +243,17 @@ def tile_crossattentionfusion_pa_kernel(tc, hsi, msi, att1, att2, wg, bg, wp, bp
                 q = m // PACK
                 gate_tile(b, m, gate[(b, q)], diff[(b, q)], att_raw[(b, q)])
 
-        x_raw[(0, 0)] = load_x(hsi, 0)
-        x_raw[(0, 1)] = load_x(msi, 0)
+        x_raw[(0, 0)] = load_x(hsi, 0, 2)
+        x_raw[(0, 1)] = load_x(msi, 0, 1)
         wg_raw[0] = load_rows(wg_view[:, 0:1, :], 1)
         wg_raw[1] = load_rows(wg_view[:, 1:2, :], 1)
         att_raw[(0, 0)] = load_att(0, 0)
         wg_raw[2] = load_rows(wg_view[:, 2:3, :], 1)
         wg_raw[3] = load_rows(wg_view[:, 3:4, :], 1)
-        x_raw[(1, 0)] = load_x(hsi, 1)
+        x_raw[(1, 0)] = load_x(hsi, 1, 1)
 
         prepare_x(x_raw[(0, 0)], 0, 0)
-        x_raw[(1, 1)] = load_x(msi, 1)
+        x_raw[(1, 1)] = load_x(msi, 1, 1)
         prepare_x(x_raw[(0, 1)], 0, 2)
         att_raw[(0, 1)] = load_att(0, 1)
         wg_chunk(0)

@@ -24,7 +24,7 @@ GROUP = PACK * PIXELS
 CHUNK = 2 * GROUP
 BANK_WORDS = 512
 PAIR = 2
-RUN = 4
+RUN = 8
 
 X_VECTOR_PIXELS = (320, 128)
 

@@ -146,7 +146,7 @@ def tile_crossattentionfusion_pa_kernel(tc, hsi, msi, att1, att2, wg, bg, wp, bp
                                     op=ALU.subtract)
             return diff
 
-        def gate_tile(b, m, gate, diff, att_raw):
+        def gate_sigmoid(b, m, gate):
             acc = psum.tile([P, PIXELS], F32, name="bank")
             for g in range(GATE_PASSES):
                 w_cols = slice((m * GATE_PASSES + g) * P, (m * GATE_PASSES + g + 1) * P)
@@ -157,6 +157,11 @@ def tile_crossattentionfusion_pa_kernel(tc, hsi, msi, att1, att2, wg, bg, wp, bp
                                     rhs=x_codes[:, x_cols].bitcast(FP8X4),
                                     rhs_scale=x_scales[:, x_cols],
                                     start=(g == 0), stop=(g == GATE_PASSES - 1))
+            first = (m % PACK) * PIXELS
+            nc.scalar.activation(out=gate[:, first:first + PIXELS], in_=acc[:], func=ACT.Sigmoid,
+                                 bias=bg_f[:, m:m + 1], scale=1.0)
+
+        def gate_product(m, gate, diff, att_raw):
             first = (m % PACK) * PIXELS
             cols = slice(first, first + PIXELS)
             if diff is None:
@@ -169,8 +174,6 @@ def tile_crossattentionfusion_pa_kernel(tc, hsi, msi, att1, att2, wg, bg, wp, bp
                 difference_of_tile = diff_bank[:]
             else:
                 difference_of_tile = diff[:, cols]
-            nc.scalar.activation(out=gate[:, cols], in_=acc[:], func=ACT.Sigmoid,
-                                 bias=bg_f[:, m:m + 1], scale=1.0)
             nc.vector.tensor_tensor(out=gate[:, cols], in0=gate[:, cols], in1=difference_of_tile,
                                     op=ALU.mult)
 
@@ -238,10 +241,16 @@ def tile_crossattentionfusion_pa_kernel(tc, hsi, msi, att1, att2, wg, bg, wp, bp
             diff[(b, q)] = difference(att_raw[(b, q)]) if q == 0 else None
             gate[(b, q)] = gates.tile([P, GROUP], F32, name="gate")
 
-        def gate_tiles(b, tiles):
+        def gate_tiles(b, tiles, products_last=False):
             for m in tiles:
                 q = m // PACK
-                gate_tile(b, m, gate[(b, q)], diff[(b, q)], att_raw[(b, q)])
+                gate_sigmoid(b, m, gate[(b, q)])
+                if not products_last:
+                    gate_product(m, gate[(b, q)], diff[(b, q)], att_raw[(b, q)])
+            if products_last:
+                for m in tiles:
+                    q = m // PACK
+                    gate_product(m, gate[(b, q)], diff[(b, q)], att_raw[(b, q)])
 
         x_raw[(0, 0)] = load_x(hsi, 0, 2)
         x_raw[(0, 1)] = load_x(msi, 0, 1)
@@ -273,7 +282,7 @@ def tile_crossattentionfusion_pa_kernel(tc, hsi, msi, att1, att2, wg, bg, wp, bp
         prepare_x(x_raw[(1, 0)], 1, 0)
         prepare_x(x_raw[(1, 1)], 1, 2)
         start_group(0, 1)
-        gate_tiles(0, (4, 5, 6, 7))
+        gate_tiles(0, (4, 5, 6, 7), True)
         blend(0, 1, gate[(0, 1)], att_raw[(0, 1)])
 
         start_group(1, 0)

from contextlib import ExitStack

import concourse.mybir as mybir
from concourse.masks import make_identity

BF16 = mybir.dt.bfloat16
F32 = mybir.dt.float32
U32 = mybir.dt.uint32
U8 = mybir.dt.uint8
FP8X4 = mybir.dt.float8_e4m3fn_x4
ALU = mybir.AluOpType
ACT = mybir.ActivationFunctionType

P = 128
PACK = 4
K_PASS = P * PACK
BATCH = 2
C = 1024
PIXELS = 512
GATE_PASSES = 2 * C // K_PASS
PROJ_PASSES = C // K_PASS
TILES = C // P
GROUP = PACK * PIXELS
CHUNK = 2 * GROUP
BANK_WORDS = 512
PAIR = 2
RUN = 8

X_VECTOR_PIXELS = (320, 128)

RAW_BUFS = 8
STAGE_BUFS = 3
GATE_BUFS = 3
DIFF_BUFS = 2
RESULT_BUFS = 4
PSUM_BANKS = 8

FLOPS = 2 * BATCH * PIXELS * (C * 2 * C + C * C)


def tile_crossattentionfusion_pa_kernel(tc, hsi, msi, att1, att2, wg, bg, wp, bp, out):
    nc = tc.nc
    with ExitStack() as ctx:
        const = ctx.enter_context(tc.tile_pool(name="const", bufs=1))
        keep = ctx.enter_context(tc.tile_pool(name="keep", bufs=1))
        raw_pool = ctx.enter_context(tc.tile_pool(name="raw", bufs=RAW_BUFS))
        stage = ctx.enter_context(tc.tile_pool(name="stage", bufs=STAGE_BUFS))
        gates = ctx.enter_context(tc.tile_pool(name="gates", bufs=GATE_BUFS))
        diffs = ctx.enter_context(tc.tile_pool(name="diffs", bufs=DIFF_BUFS))
        results = ctx.enter_context(tc.tile_pool(name="results", bufs=RESULT_BUFS))
        psum = ctx.enter_context(tc.psum_pool(name="psum", bufs=PSUM_BANKS))

        ident = const.tile([P, P], F32)
        make_identity(nc, ident[:])
        plus = const.tile([P, P], BF16)
        make_identity(nc, plus[:])
        minus = const.tile([P, P], BF16)
        nc.vector.tensor_scalar(out=minus[:], in0=plus[:], scalar1=-1.0, scalar2=None, op0=ALU.mult)
        bg_rows = const.tile([P, P], F32)
        nc.vector.memset(bg_rows[:], 0.0)
        nc.scalar.dma_start(out=bg_rows[0:TILES // PAIR, :].bitcast(BF16),
                            in_=bg.rearrange("(a w) -> a w", a=TILES // PAIR))
        bg_bank = psum.tile([P, P], F32, name="bank")
        nc.tensor.transpose(bg_bank[:], bg_rows[:], ident[:])
        bg_bf = const.tile([P, TILES], BF16)
        nc.vector.tensor_copy(out=bg_bf[:].bitcast(F32), in_=bg_bank[:, 0:TILES // PAIR])
        bp_bf = const.tile([P, TILES], BF16)
        warm = const.tile([P, 1], F32)
        nc.vector.memset(warm[:], 0.0)
        warm_out = const.tile([P, 1], F32)
        nc.scalar.activation(out=warm_out[:], in_=warm[:], func=ACT.Sigmoid)
        bg_f = const.tile([P, TILES], F32)
        nc.vector.tensor_copy(out=bg_f[:], in_=bg_bf[:])
        bp_f = const.tile([P, TILES], F32)

        wg_codes = keep.tile([P, TILES * GATE_PASSES * P], U32, align_bytes=64)
        wg_scales = keep.tile([P, TILES * GATE_PASSES * P], U8, align_bytes=64)
        wp_codes = keep.tile([P, TILES * PROJ_PASSES * P], U32, align_bytes=64)
        wp_scales = keep.tile([P, TILES * PROJ_PASSES * P], U8, align_bytes=64)
        x_codes = keep.tile([P, BATCH * GATE_PASSES * PIXELS], U32, align_bytes=64)
        x_scales = keep.tile([P, BATCH * GATE_PASSES * PIXELS], U8, align_bytes=64)
        f_codes = keep.tile([P, BATCH * PROJ_PASSES * PIXELS], U32, align_bytes=64)
        f_scales = keep.tile([P, BATCH * PROJ_PASSES * PIXELS], U8, align_bytes=64)

        def load_rows(view, pieces):
            raw = raw_pool.tile([P, CHUNK], BF16, name="raw")
            runs = view.shape[1]
            raw_view = raw[:].rearrange("p (a f) -> p a f", a=runs)
            step = runs // pieces
            for i in range(pieces):
                nc.sync.dma_start(out=raw_view[:, i * step:(i + 1) * step, :],
                                  in_=view[:, i * step:(i + 1) * step, :])
            return raw

        def map_view(feature_map, b):
            return feature_map[b].rearrange("(a p e) h w -> p a (e h w)", p=P, e=PAIR)

        def load_x(feature_map, b, pieces):
            return load_rows(map_view(feature_map, b), pieces)

        def load_att(b, q):
            raw = raw_pool.tile([P, CHUNK], BF16, name="raw")
            for i, feature_map in enumerate((att1, att2)):
                nc.sync.dma_start(
                    out=raw[:, i * GROUP:(i + 1) * GROUP].rearrange("p (a f) -> p a f", a=PAIR),
                    in_=map_view(feature_map, b)[:, PAIR * q:PAIR * q + PAIR, :])
            return raw

        def prepare_weights(raw, codes, scales):
            words = raw[:].bitcast(F32)
            for half in range(2):
                grouped = stage.tile([P, CHUNK // 2], BF16, name="w_grouped", align_bytes=64)
                grouped_words = grouped[:].bitcast(F32)
                for j in range(2):
                    first = (2 * half + j) * BANK_WORDS
                    bank = psum.tile([P, BANK_WORDS], F32, name="bank")
                    for i in range(BANK_WORDS // P):
                        nc.tensor.transpose(bank[:, i * P:(i + 1) * P],
                                            words[:, first + i * P:first + (i + 1) * P], ident[:])
                    dst = grouped_words[:, j * BANK_WORDS:(j + 1) * BANK_WORDS].rearrange(
                        "p (a c u) -> p a c u", a=2, u=PAIR)
                    src = bank[:].rearrange("p (a u c) -> p a c u", a=2, u=PAIR)
                    nc.scalar.copy(out=dst, in_=src)
                cols = slice(half * BANK_WORDS, (half + 1) * BANK_WORDS)
                nc.vector.quantize_mx(out=codes[:, cols].bitcast(FP8X4), scales=scales[:, cols],
                                      in_=grouped[:])

        def prepare_x(raw, b, first_pass):
            grouped = []
            for g in range(2):
                src = raw[:, g * GROUP:(g + 1) * GROUP].rearrange(
                    "p (t c i) -> p c t i", t=PACK, i=RUN)
                grouped.append(stage.tile([P, GROUP], BF16, name="x_grouped", align_bytes=64))
                dst = grouped[g][:].rearrange("p (c i t) -> p c t i", i=RUN, t=PACK)
                cut = X_VECTOR_PIXELS[b] // RUN
                nc.vector.tensor_copy(out=dst[:, :cut], in_=src[:, :cut])
                nc.scalar.copy(out=dst[:, cut:], in_=src[:, cut:])
            for g in range(2):
                first = (b * GATE_PASSES + first_pass + g) * PIXELS
                nc.vector.quantize_mx(out=x_codes[:, first:first + PIXELS].bitcast(FP8X4),
                                      scales=x_scales[:, first:first + PIXELS], in_=grouped[g][:])

        def difference(att_raw):
            diff = diffs.tile([P, GROUP], F32, name="diff")
            nc.vector.tensor_tensor(out=diff[:], in0=att_raw[:, :GROUP], in1=att_raw[:, GROUP:],
                                    op=ALU.subtract)
            return diff

        def gate_sigmoid(b, m, gate):
            acc = psum.tile([P, PIXELS], F32, name="bank")
            for g in range(GATE_PASSES):
                w_cols = slice((m * GATE_PASSES + g) * P, (m * GATE_PASSES + g + 1) * P)
                x_cols = slice((b * GATE_PASSES + g) * PIXELS, (b * GATE_PASSES + g + 1) * PIXELS)
                nc.tensor.matmul_mx(out=acc[:],
                                    lhsT=wg_codes[:, w_cols].bitcast(FP8X4),
                                    lhsT_scale=wg_scales[:, w_cols],
                                    rhs=x_codes[:, x_cols].bitcast(FP8X4),
                                    rhs_scale=x_scales[:, x_cols],
                                    start=(g == 0), stop=(g == GATE_PASSES - 1))
            first = (m % PACK) * PIXELS
            nc.scalar.activation(out=gate[:, first:first + PIXELS], in_=acc[:], func=ACT.Sigmoid,
                                 bias=bg_f[:, m:m + 1], scale=1.0)

        def gate_product(m, gate, diff, att_raw):
            first = (m % PACK) * PIXELS
            cols = slice(first, first + PIXELS)
            if diff is None:
                diff_bank = psum.tile([P, PIXELS], F32, name="bank")
                nc.tensor.matmul(out=diff_bank[:], lhsT=plus[:], rhs=att_raw[:, cols],
                                 start=True, stop=False)
                nc.tensor.matmul(out=diff_bank[:], lhsT=minus[:],
                                 rhs=att_raw[:, GROUP + first:GROUP + first + PIXELS],
                                 start=False, stop=True)
                difference_of_tile = diff_bank[:]
            else:
                difference_of_tile = diff[:, cols]
            nc.vector.tensor_tensor(out=gate[:, cols], in0=gate[:, cols], in1=difference_of_tile,
                                    op=ALU.mult)

        def blend(b, q, gate, att_raw):
            fused = stage.tile([P, GROUP], BF16, name="f_grouped", align_bytes=64)
            fused_view = fused[:].rearrange("p (c i t) -> p c t i", i=RUN, t=PACK)
            gate_view = gate[:].rearrange("p (t c i) -> p c t i", t=PACK, i=RUN)
            att2_view = att_raw[:, GROUP:].rearrange("p (t c i) -> p c t i", t=PACK, i=RUN)
            runs = PIXELS // RUN // 2
            for h in range(2):
                part = slice(h * runs, (h + 1) * runs)
                nc.vector.tensor_tensor(out=fused_view[:, part], in0=gate_view[:, part],
                                        in1=att2_view[:, part], op=ALU.add)
            for h in range(2):
                first = (b * PROJ_PASSES + q) * PIXELS + h * PIXELS // 2
                cols = slice(first, first + PIXELS // 2)
                nc.vector.quantize_mx(out=f_codes[:, cols].bitcast(FP8X4), scales=f_scales[:, cols],
                                      in_=fused[:, h * GROUP // 2:(h + 1) * GROUP // 2])

        def project(b, vector_helps):
            out_view = out[b].rearrange("(p j) h w -> p (j h w)", j=TILES)
            for pair in range(TILES // 2):
                result = results.tile([P, 2 * PIXELS], F32, name="result")
                for i in range(2):
                    j = 2 * pair + i
                    acc = psum.tile([P, PIXELS], F32, name="bank")
                    for q in range(PROJ_PASSES):
                        w_cols = slice((j * PROJ_PASSES + q) * P, (j * PROJ_PASSES + q + 1) * P)
                        f_cols = slice((b * PROJ_PASSES + q) * PIXELS,
                                       (b * PROJ_PASSES + q + 1) * PIXELS)
                        nc.tensor.matmul_mx(out=acc[:],
                                            lhsT=wp_codes[:, w_cols].bitcast(FP8X4),
                                            lhsT_scale=wp_scales[:, w_cols],
                                            rhs=f_codes[:, f_cols].bitcast(FP8X4),
                                            rhs_scale=f_scales[:, f_cols],
                                            start=(q == 0), stop=(q == PROJ_PASSES - 1))
                    cols = slice(i * PIXELS, (i + 1) * PIXELS)
                    if vector_helps and i == 1:
                        nc.vector.tensor_scalar(out=result[:, cols], in0=acc[:],
                                                scalar1=bp_f[:, j:j + 1], scalar2=None, op0=ALU.add)
                    else:
                        nc.scalar.activation(out=result[:, cols], in_=acc[:], func=ACT.Identity,
                                             bias=bp_f[:, j:j + 1], scale=1.0)
                nc.sync.dma_start(out=out_view[:, pair * 2 * PIXELS:(pair + 1) * 2 * PIXELS],
                                  in_=result[:])

        wg_view = wg.rearrange("(a p e) k -> p a (e k)", p=P, e=PAIR)
        wp_view = wp.rearrange("(p h j) k -> p h (j k)", h=2, j=TILES // 2)
        x_raw = {}
        wg_raw = {}
        wp_raw = {}
        att_raw = {}
        diff = {}
        gate = {}

        def wg_chunk(a):
            cols = slice(a * CHUNK // PACK, (a + 1) * CHUNK // PACK)
            prepare_weights(wg_raw[a], wg_codes[:, cols], wg_scales[:, cols])

        def wp_chunk(h):
            cols = slice(h * CHUNK // PACK, (h + 1) * CHUNK // PACK)
            prepare_weights(wp_raw[h], wp_codes[:, cols], wp_scales[:, cols])

        def start_group(b, q):
            diff[(b, q)] = difference(att_raw[(b, q)]) if q == 0 else None
            gate[(b, q)] = gates.tile([P, GROUP], F32, name="gate")

        def gate_tiles(b, tiles, products_last=False):
            for m in tiles:
                q = m // PACK
                gate_sigmoid(b, m, gate[(b, q)])
                if not products_last:
                    gate_product(m, gate[(b, q)], diff[(b, q)], att_raw[(b, q)])
            if products_last:
                for m in tiles:
                    q = m // PACK
                    gate_product(m, gate[(b, q)], diff[(b, q)], att_raw[(b, q)])

        x_raw[(0, 0)] = load_x(hsi, 0, 2)
        x_raw[(0, 1)] = load_x(msi, 0, 1)
        wg_raw[0] = load_rows(wg_view[:, 0:1, :], 1)
        wg_raw[1] = load_rows(wg_view[:, 1:2, :], 1)
        att_raw[(0, 0)] = load_att(0, 0)
        wg_raw[2] = load_rows(wg_view[:, 2:3, :], 1)
        wg_raw[3] = load_rows(wg_view[:, 3:4, :], 1)
        x_raw[(1, 0)] = load_x(hsi, 1, 1)

        prepare_x(x_raw[(0, 0)], 0, 0)
        x_raw[(1, 1)] = load_x(msi, 1, 1)
        prepare_x(x_raw[(0, 1)], 0, 2)
        att_raw[(0, 1)] = load_att(0, 1)
        wg_chunk(0)
        att_raw[(1, 0)] = load_att(1, 0)
        wg_chunk(1)
        att_raw[(1, 1)] = load_att(1, 1)
        start_group(0, 0)
        gate_tiles(0, (0, 1))
        wg_chunk(2)
        wp_raw[0] = load_rows(wp_view[:, 0:1, :], 1)
        gate_tiles(0, (2, 3))
        wg_chunk(3)
        wp_raw[1] = load_rows(wp_view[:, 1:2, :], 1)
        nc.sync.dma_start(out=bp_bf[:], in_=bp.rearrange("(p j) -> p j", j=TILES))
        nc.vector.tensor_copy(out=bp_f[:], in_=bp_bf[:])
        blend(0, 0, gate[(0, 0)], att_raw[(0, 0)])
        prepare_x(x_raw[(1, 0)], 1, 0)
        prepare_x(x_raw[(1, 1)], 1, 2)
        start_group(0, 1)
        gate_tiles(0, (4, 5, 6, 7), True)
        blend(0, 1, gate[(0, 1)], att_raw[(0, 1)])

        start_group(1, 0)
        gate_tiles(1, (0, 1, 2, 3))
        wp_chunk(0)
        wp_chunk(1)
        blend(1, 0, gate[(1, 0)], att_raw[(1, 0)])
        start_group(1, 1)
        gate_tiles(1, (4, 5, 6, 7))
        project(0, False)
        blend(1, 1, gate[(1, 1)], att_raw[(1, 1)])
        project(1, True)
